import numpy as np
import ml_dtypes


def mxq(x, axis, fmt="e4m3"):
    dtype, down = {"e4m3": (ml_dtypes.float8_e4m3fn, 7), "e5m2": (ml_dtypes.float8_e5m2, 14)}[fmt]
    v = np.moveaxis(np.asarray(x, np.float32).astype(ml_dtypes.bfloat16).astype(np.float64), axis, -1)
    blocks = v.reshape(v.shape[:-1] + (-1, 32))
    amax = np.abs(blocks).max(-1, keepdims=True)
    byte = np.maximum(np.where(amax > 0, np.frexp(amax)[1] - 1 + 127, 0) - down, 1)
    scale = np.exp2(byte - 127.0)
    codes = (blocks / scale).astype(np.float32).astype(dtype).astype(np.float64)
    return np.moveaxis((codes * scale).reshape(v.shape), -1, axis)


WIDE = False


def mx_kscale(k):
    if not WIDE:
        return np.ones(k)
    levels = np.array([10, -10, 5, -5, 0])
    a = np.random.permutation(np.resize(levels, k // 512 * 4)).reshape(k // 512, 4)
    idx = np.arange(k)
    return np.exp2(a[idx // 512, idx % 128 // 32])


BF16 = ml_dtypes.bfloat16


def bf(x):
    return np.asarray(x, np.float32).astype(BF16)


def f64(x):
    return np.asarray(x).astype(np.float64)


B, D, H = 4096, 1024, 512
HALF = D // 2


def setup_inputs():
    us, ut = mx_kscale(H), mx_kscale(H)
    return {
        "z": bf(np.random.standard_normal((B, D))),
        "W1_s": bf(np.random.standard_normal((HALF, H)) / np.sqrt(HALF) * us),
        "b1_s": bf(np.random.standard_normal(H) * 0.3 * us),
        "W2_s": bf(np.random.standard_normal((H, HALF)) * 0.5 / np.sqrt(H) / us[:, None]),
        "b2_s": bf(np.random.standard_normal(HALF) * 0.1),
        "W1_t": bf(np.random.standard_normal((HALF, H)) / np.sqrt(HALF) * ut),
        "b1_t": bf(np.random.standard_normal(H) * 0.3 * ut),
        "W2_t": bf(np.random.standard_normal((H, HALF)) / np.sqrt(H) / ut[:, None]),
        "b2_t": bf(np.random.standard_normal(HALF) * 0.3),
    }


def reference(z, W1_s, b1_s, W2_s, b2_s, W1_t, b1_t, W2_t, b2_t):
    z = f64(z)
    a = z[:, 0::2]
    b = z[:, 1::2]
    aq = mxq(a, 1, "e4m3")
    hs = np.maximum((aq @ mxq(f64(W1_s), 0, "e4m3")) + f64(b1_s), 0.0)
    s = (mxq(hs, 1, "e4m3") @ mxq(f64(W2_s), 0, "e4m3")) + f64(b2_s)
    ht = np.maximum((aq @ mxq(f64(W1_t), 0, "e4m3")) + f64(b1_t), 0.0)
    t = (mxq(ht, 1, "e4m3") @ mxq(f64(W2_t), 0, "e4m3")) + f64(b2_t)
    b_out = b * np.exp(s) + t
    logdet = s.sum(axis=1)
    z_out = np.stack([a, b_out], axis=2).reshape(B, D)
    return z_out, logdet

@@ -1,0 +1,297 @@
+from contextlib import ExitStack
+
+import concourse.mybir as mybir
+from concourse.masks import make_identity
+
+FLOPS = 4 * 2 * 4096 * 512 * 512
+
+FP8X4 = mybir.dt.float8_e4m3fn_x4
+BF16 = mybir.dt.bfloat16
+F32 = mybir.dt.float32
+U32 = mybir.dt.uint32
+U8 = mybir.dt.uint8
+ACT = mybir.ActivationFunctionType
+ALU = mybir.AluOpType
+
+P = 128
+D = 1024
+HALF = 512
+NT = 32
+RT = 4
+ST = NT // RT
+NM2 = 4
+LAG_B = 5
+LAG_C1 = 9
+LAG_C2 = 11
+
+
+def tile_affinecoupling_pa_t_kernel(
+    tc, z, W1_s, b1_s, W2_s, b2_s, W1_t, b1_t, W2_t, b2_t, out_0, out_1
+):
+    nc = tc.nc
+    zv = z.rearrange("(p i) d -> p i d", i=NT)
+    ov = out_0.rearrange("(p i) d -> p i d", i=NT)
+    ldv = out_1.rearrange("(p i) -> p i", i=NT)
+
+    with ExitStack() as ctx:
+        ctx.enter_context(tc.manual_schedule())
+        const = ctx.enter_context(tc.tile_pool(name="const", bufs=1))
+        wraw_pool = ctx.enter_context(tc.tile_pool(name="wraw", bufs=4))
+        two = ctx.enter_context(tc.tile_pool(name="two", bufs=2))
+        three = ctx.enter_context(tc.tile_pool(name="three", bufs=3))
+        ptp = ctx.enter_context(tc.psum_pool(name="ptp", bufs=2))
+        ph = ctx.enter_context(tc.psum_pool(name="ph", bufs=2))
+        ps = ctx.enter_context(tc.psum_pool(name="ps", bufs=2))
+        pat = ctx.enter_context(tc.psum_pool(name="pat", bufs=2))
+
+        ident_f = const.tile([P, P], F32, name="ident_f")
+        make_identity(nc, ident_f[:])
+        ident_b = const.tile([P, P], BF16, name="ident_b")
+        make_identity(nc, ident_b[:])
+        m2s = []
+        for i in range(NM2):
+            m2 = const.tile([P, 2, 2, 256], F32, name="m2_%d" % i)
+            nc.gpsimd.memset(m2[:], 0.0)
+            m2s.append(m2)
+
+        bt = const.tile([P, P], BF16, name="bt")
+        nc.vector.memset(bt[:], 0.0)
+
+        z_sb = []
+        for n in range(ST):
+            zt = const.tile([P, RT * D], BF16, name="z%d" % n)
+            z_sb.append(zt)
+
+        def load_z(n, lo, hi):
+            nc.sync.dma_start(
+                out=z_sb[n][:, lo * D : hi * D].rearrange("p (i d) -> p i d", d=D),
+                in_=zv[:, n * RT + lo : n * RT + hi, :],
+            )
+
+        def load_w(w):
+            raw = wraw_pool.tile([P, 4, 512], BF16, tag="wraw")
+            nc.sync.dma_start(out=raw[:], in_=w.rearrange("(c p) n -> p c n", p=P))
+            return raw
+
+        b2raw = const.tile([P, 2, 512], BF16, name="b2raw")
+        load_z(0, 0, 2)
+        raw_w1s = load_w(W1_s)
+        load_z(0, 2, 4)
+        raw_w1t = load_w(W1_t)
+        nc.sync.dma_start(out=bt[0:4, :], in_=b1_s.rearrange("(t p) -> t p", p=P))
+        nc.sync.dma_start(out=bt[4:8, :], in_=b1_t.rearrange("(t p) -> t p", p=P))
+        load_z(1, 0, 4)
+        raw_w2s = load_w(W2_s)
+        raw_w2t = load_w(W2_t)
+        nc.sync.dma_start(out=b2raw[:, 0, :], in_=b2_s.partition_broadcast(P))
+        nc.sync.dma_start(out=b2raw[:, 1, :], in_=b2_t.partition_broadcast(P))
+        for n in range(2, ST):
+            load_z(n, 0, 4)
+
+        zw = [t[:].bitcast(F32) for t in z_sb]
+        zq = [
+            t[:].rearrange("p (r h j e) -> p r e h j", r=RT, h=2, j=256, e=2)
+            for t in z_sb
+        ]
+
+        w1cod = const.tile([P, 1024], U32, name="w1cod", align_bytes=64)
+        w1scl = const.tile([P, 1024], U8, name="w1scl", align_bytes=64)
+        w2cod = const.tile([P, 1024], U32, name="w2cod", align_bytes=64)
+        w2scl = const.tile([P, 1024], U8, name="w2scl", align_bytes=64)
+        b1 = const.tile([P, 8], F32, name="b1")
+        b2f = const.tile([P, 2, 512], F32, name="b2f")
+        ld = const.tile([P, NT], F32, name="ld")
+
+        def regroup(dst, src):
+            nc.vector.tensor_copy(
+                out=dst[:].rearrange("p (c i) t -> p c t i", i=4),
+                in_=src[:].rearrange("p t (c i) -> p c t i", i=4),
+            )
+
+        def quant(cod, scl, grp):
+            nc.vector.quantize_mx(
+                out=cod.bitcast(FP8X4),
+                scales=scl,
+                in_=grp[:].rearrange("p w t -> p (w t)"),
+            )
+
+        wg = {}
+
+        def w_regroup(key, raw):
+            grp = two.tile([P, 512, 4], BF16, tag="wgrp", align_bytes=64)
+            regroup(grp, raw)
+            wg[key] = grp
+
+        w_regroup("w1s", raw_w1s)
+        w_regroup("w1t", raw_w1t)
+        quant(w1cod[:, 0:512], w1scl[:, 0:512], wg["w1s"])
+        quant(w1cod[:, 512:1024], w1scl[:, 512:1024], wg["w1t"])
+
+        ags, acods, hpls, hgs, hcods, zos = {}, {}, {}, {}, {}, {}
+
+        def stage_a(n, k):
+            tp = ptp.tile([P, 512], F32, tag="tp")
+            for c in range(4):
+                nc.tensor.transpose(
+                    tp[:, c * P : (c + 1) * P],
+                    zw[n][:, k * 512 + c * P : k * 512 + (c + 1) * P],
+                    ident_f[:],
+                )
+            if k == 0:
+                ag = two.tile([P, 512, 4], BF16, tag="ag", align_bytes=64)
+                ags[n] = ag
+            src = tp[:].bitcast(BF16).rearrange("p (c w e) -> p e w c", c=4, w=P, e=2)
+            nc.scalar.copy(out=ags[n][:, k * P : (k + 1) * P, :], in_=src[:, 0])
+
+        def quant_a(n):
+            acod = two.tile([P, 512], U32, tag="acod", align_bytes=64)
+            ascl = two.tile([P, 512], U8, tag="ascl", align_bytes=64)
+            quant(acod[:], ascl[:], ags[n])
+            acods[n] = (acod, ascl)
+
+        def stage_b(n, k):
+            acod, ascl = acods[n]
+            for m in (2 * k, 2 * k + 1):
+                br, t = m // 4, m % 4
+                if t == 0:
+                    hpl = two.tile([P, 4, 512], BF16, tag="hpl%d" % br)
+                    hpls[(n, br)] = hpl
+                hps = ph.tile([P, 512], F32, tag="h")
+                nc.tensor.matmul_mx(
+                    out=hps[:],
+                    lhsT=w1cod[:, m * P : (m + 1) * P].bitcast(FP8X4),
+                    lhsT_scale=w1scl[:, m * P : (m + 1) * P],
+                    rhs=acod[:].bitcast(FP8X4),
+                    rhs_scale=ascl[:],
+                    start=True,
+                    stop=True,
+                )
+                nc.scalar.activation(
+                    out=hpls[(n, br)][:, t, :],
+                    in_=hps[:],
+                    func=ACT.Relu,
+                    bias=b1[:, m : m + 1],
+                    scale=1.0,
+                )
+
+        def regroup_h(n, br):
+            hg = two.tile([P, 512, 4], BF16, tag="hg%d" % br, align_bytes=64)
+            regroup(hg, hpls[(n, br)])
+            hgs[(n, br)] = hg
+
+        def quant_h(n, br):
+            hcod = two.tile([P, 512], U32, tag="hcod%d" % br, align_bytes=64)
+            hscl = two.tile([P, 512], U8, tag="hscl%d" % br, align_bytes=64)
+            quant(hcod[:], hscl[:], hgs[(n, br)])
+            hcods[(n, br)] = (hcod, hscl)
+
+        def stage_c1(n, k):
+            i = n * RT + k
+            hcod, hscl = hcods[(n, 0)]
+            sps = ps.tile([P, 512], F32, tag="s")
+            nc.tensor.matmul_mx(
+                out=sps[:],
+                lhsT=hcod[:, k * P : (k + 1) * P].bitcast(FP8X4),
+                lhsT_scale=hscl[:, k * P : (k + 1) * P],
+                rhs=w2cod[:, 0:512].bitcast(FP8X4),
+                rhs_scale=w2scl[:, 0:512],
+                start=True,
+                stop=True,
+            )
+            sp = three.tile([P, 512], F32, tag="sp")
+            nc.vector.scalar_tensor_tensor(
+                out=sp[:],
+                in0=sps[:],
+                scalar=1.0,
+                in1=b2f[:, 0, :],
+                op0=ALU.mult,
+                op1=ALU.add,
+                accum_out=ld[:, i : i + 1],
+            )
+            m2 = m2s[i % NM2]
+            nc.scalar.activation(
+                out=m2[:, :, 1, :],
+                in_=sp[:].rearrange("p (h j) -> p h j", h=2),
+                func=ACT.Exp,
+            )
+            nc.gpsimd.tensor_tensor(
+                out=m2[:, :, 1, :], in0=m2[:, :, 1, :], in1=zq[n][:, k, 1], op=ALU.mult
+            )
+            nc.gpsimd.tensor_tensor(
+                out=m2[:, :, 1, :],
+                in0=m2[:, :, 1, :],
+                in1=b2f[:, 1, :].rearrange("p (h j) -> p h j", h=2),
+                op=ALU.add,
+            )
+
+        def stage_c2(n, k):
+            i = n * RT + k
+            hcod, hscl = hcods[(n, 1)]
+            m2 = m2s[i % NM2]
+            if k == 0:
+                zo = two.tile([P, RT, D], F32, tag="zo")
+                zos[n] = zo
+            ats = []
+            for h in range(2):
+                at = pat.tile([P, 2, 256], F32, tag="at")
+                ats.append(at)
+                nc.tensor.matmul(
+                    out=at[:, 0, :], lhsT=ident_b[:], rhs=zq[n][:, k, 0, h], start=True, stop=True
+                )
+            for h in range(2):
+                nc.tensor.matmul_mx(
+                    out=ats[h][:, 1, :],
+                    lhsT=hcod[:, k * P : (k + 1) * P].bitcast(FP8X4),
+                    lhsT_scale=hscl[:, k * P : (k + 1) * P],
+                    rhs=w2cod[:, 512 + h * 256 : 512 + (h + 1) * 256].bitcast(FP8X4),
+                    rhs_scale=w2scl[:, 512 + h * 256 : 512 + (h + 1) * 256],
+                    start=True,
+                    stop=True,
+                )
+            for h in range(2):
+                nc.vector.tensor_tensor(
+                    out=zos[n][:, k, h * 512 : (h + 1) * 512].rearrange("p (j e) -> p j e", e=2),
+                    in0=ats[h][:].rearrange("p e j -> p j e"),
+                    in1=m2[:, h].rearrange("p e j -> p j e"),
+                    op=ALU.add,
+                )
+            if k == RT - 1:
+                nc.sync.dma_start(out=ov[:, n * RT : (n + 1) * RT, :], in_=zos[n][:])
+
+        nslots = NT + LAG_C2
+        for q in range(nslots):
+            if q < NT:
+                stage_a(q // RT, q % RT)
+            if q == 2:
+                btp = ptp.tile([P, P], BF16, tag="tp")
+                nc.tensor.transpose(btp[:], bt[:], ident_b[:])
+                nc.vector.tensor_copy(out=b1[:], in_=btp[:, 0:8])
+            if q >= 4 and q % RT == 0 and q // RT - 1 < ST:
+                quant_a(q // RT - 1)
+            if q == 4:
+                w_regroup("w2s", raw_w2s)
+            if q == 5:
+                w_regroup("w2t", raw_w2t)
+                quant(w2cod[:, 0:512], w2scl[:, 0:512], wg["w2s"])
+            if q == 6:
+                quant(w2cod[:, 512:1024], w2scl[:, 512:1024], wg["w2t"])
+                nc.vector.tensor_copy(out=b2f[:], in_=b2raw[:])
+            qb = q - LAG_B
+            if 0 <= qb < NT:
+                stage_b(qb // RT, qb % RT)
+            qc = q - LAG_C1
+            if 0 <= qc < NT:
+                stage_c1(qc // RT, qc % RT)
+            qd = q - LAG_C2
+            if 0 <= qd < NT:
+                stage_c2(qd // RT, qd % RT)
+            if 0 <= qb < NT and qb % RT == 1:
+                regroup_h(qb // RT, 0)
+            if 0 <= qb < NT and qb % RT == 2:
+                quant_h(qb // RT, 0)
+            if 0 <= qb < NT and qb % RT == 3:
+                regroup_h(qb // RT, 1)
+            if 0 <= qb - 1 < NT and (qb - 1) % RT == 3:
+                quant_h((qb - 1) // RT, 1)
+
+        nc.sync.dma_start(out=ldv, in_=ld[:])

@@ -15,14 +15,16 @@ ALU = mybir.AluOpType
 
 P = 128
 D = 1024
-HALF = 512
 NT = 32
 RT = 4
 ST = NT // RT
 NM2 = 4
-LAG_B = 5
-LAG_C1 = 9
-LAG_C2 = 11
+
+LAG = {
+    "tr": 0, "aev": 0, "QA": 1, "W": 4, "mx1": 5, "relu": 5, "RG": 5, "QH": 6,
+    "mxT": 8, "tev": 8, "mxs": 10, "sp": 10, "exp": 10, "M": 11, "at": 13, "fin": 13,
+}
+ORDER = ["QA", "at", "tr", "mx1", "mxs", "relu", "fin", "mxT", "M", "sp", "RG", "W", "aev", "QH", "tev", "exp"]
 
 
 def tile_affinecoupling_pa_t_kernel(
@@ -36,7 +38,6 @@ def tile_affinecoupling_pa_t_kernel(
     with ExitStack() as ctx:
         ctx.enter_context(tc.manual_schedule())
         const = ctx.enter_context(tc.tile_pool(name="const", bufs=1))
-        wraw_pool = ctx.enter_context(tc.tile_pool(name="wraw", bufs=4))
         two = ctx.enter_context(tc.tile_pool(name="two", bufs=2))
         three = ctx.enter_context(tc.tile_pool(name="three", bufs=3))
         ptp = ctx.enter_context(tc.psum_pool(name="ptp", bufs=2))
@@ -68,23 +69,23 @@ def tile_affinecoupling_pa_t_kernel(
                 in_=zv[:, n * RT + lo : n * RT + hi, :],
             )
 
-        def load_w(w):
-            raw = wraw_pool.tile([P, 4, 512], BF16, tag="wraw")
+        def load_w(w, tag):
+            raw = two.tile([P, 4, 512], BF16, tag=tag)
             nc.sync.dma_start(out=raw[:], in_=w.rearrange("(c p) n -> p c n", p=P))
             return raw
 
-        b2raw = const.tile([P, 2, 512], BF16, name="b2raw")
+        b2raw = const.tile([P, 512], BF16, name="b2raw")
         load_z(0, 0, 2)
-        raw_w1s = load_w(W1_s)
+        raw_w1t = load_w(W1_t, "hpl1")
         load_z(0, 2, 4)
-        raw_w1t = load_w(W1_t)
+        raw_w1s = load_w(W1_s, "hpl0")
         nc.sync.dma_start(out=bt[0:4, :], in_=b1_s.rearrange("(t p) -> t p", p=P))
         nc.sync.dma_start(out=bt[4:8, :], in_=b1_t.rearrange("(t p) -> t p", p=P))
+        nc.sync.dma_start(out=bt[8:12, :], in_=b2_t.rearrange("(t p) -> t p", p=P))
         load_z(1, 0, 4)
-        raw_w2s = load_w(W2_s)
-        raw_w2t = load_w(W2_t)
-        nc.sync.dma_start(out=b2raw[:, 0, :], in_=b2_s.partition_broadcast(P))
-        nc.sync.dma_start(out=b2raw[:, 1, :], in_=b2_t.partition_broadcast(P))
+        raw_w2t = load_w(W2_t, "wraw")
+        raw_w2s = load_w(W2_s, "wraw")
+        nc.sync.dma_start(out=b2raw[:], in_=b2_s.partition_broadcast(P))
         for n in range(2, ST):
             load_z(n, 0, 4)
 
@@ -98,8 +99,8 @@ def tile_affinecoupling_pa_t_kernel(
         w1scl = const.tile([P, 1024], U8, name="w1scl", align_bytes=64)
         w2cod = const.tile([P, 1024], U32, name="w2cod", align_bytes=64)
         w2scl = const.tile([P, 1024], U8, name="w2scl", align_bytes=64)
-        b1 = const.tile([P, 8], F32, name="b1")
-        b2f = const.tile([P, 2, 512], F32, name="b2f")
+        bias = const.tile([P, 12], F32, name="bias")
+        b2f = const.tile([P, 512], F32, name="b2f")
         ld = const.tile([P, NT], F32, name="ld")
 
         def regroup(dst, src):
@@ -117,78 +118,114 @@ def tile_affinecoupling_pa_t_kernel(
 
         wg = {}
 
-        def w_regroup(key, raw):
-            grp = two.tile([P, 512, 4], BF16, tag="wgrp", align_bytes=64)
+        def w_regroup(key, raw, tag):
+            grp = two.tile([P, 512, 4], BF16, tag=tag, align_bytes=64)
             regroup(grp, raw)
             wg[key] = grp
 
-        w_regroup("w1s", raw_w1s)
-        w_regroup("w1t", raw_w1t)
-        quant(w1cod[:, 0:512], w1scl[:, 0:512], wg["w1s"])
+        w_regroup("w1t", raw_w1t, "hg1")
+        w_regroup("w1s", raw_w1s, "hg0")
         quant(w1cod[:, 512:1024], w1scl[:, 512:1024], wg["w1t"])
+        quant(w1cod[:, 0:512], w1scl[:, 0:512], wg["w1s"])
 
-        ags, acods, hpls, hgs, hcods, zos = {}, {}, {}, {}, {}, {}
+        tps, ags, acods, hpss, hpls, hgs, hcods, tpss, tTs, spss, sps_sb, atss, zos = (
+            {}, {}, {}, {}, {}, {}, {}, {}, {}, {}, {}, {}, {},
+        )
 
-        def stage_a(n, k):
+        def op_tr(i):
+            n, k = i // RT, i % RT
             tp = ptp.tile([P, 512], F32, tag="tp")
+            tps[i] = tp
             for c in range(4):
                 nc.tensor.transpose(
                     tp[:, c * P : (c + 1) * P],
                     zw[n][:, k * 512 + c * P : k * 512 + (c + 1) * P],
                     ident_f[:],
                 )
+
+        def op_aev(i):
+            n, k = i // RT, i % RT
             if k == 0:
                 ag = two.tile([P, 512, 4], BF16, tag="ag", align_bytes=64)
                 ags[n] = ag
-            src = tp[:].bitcast(BF16).rearrange("p (c w e) -> p e w c", c=4, w=P, e=2)
+            src = tps[i][:].bitcast(BF16).rearrange("p (c w e) -> p e w c", c=4, w=P, e=2)
             nc.scalar.copy(out=ags[n][:, k * P : (k + 1) * P, :], in_=src[:, 0])
 
-        def quant_a(n):
+        def op_qa(n):
             acod = two.tile([P, 512], U32, tag="acod", align_bytes=64)
             ascl = two.tile([P, 512], U8, tag="ascl", align_bytes=64)
             quant(acod[:], ascl[:], ags[n])
             acods[n] = (acod, ascl)
 
-        def stage_b(n, k):
+        def op_mx1(n, m):
             acod, ascl = acods[n]
-            for m in (2 * k, 2 * k + 1):
-                br, t = m // 4, m % 4
-                if t == 0:
-                    hpl = two.tile([P, 4, 512], BF16, tag="hpl%d" % br)
-                    hpls[(n, br)] = hpl
-                hps = ph.tile([P, 512], F32, tag="h")
-                nc.tensor.matmul_mx(
-                    out=hps[:],
-                    lhsT=w1cod[:, m * P : (m + 1) * P].bitcast(FP8X4),
-                    lhsT_scale=w1scl[:, m * P : (m + 1) * P],
-                    rhs=acod[:].bitcast(FP8X4),
-                    rhs_scale=ascl[:],
-                    start=True,
-                    stop=True,
-                )
-                nc.scalar.activation(
-                    out=hpls[(n, br)][:, t, :],
-                    in_=hps[:],
-                    func=ACT.Relu,
-                    bias=b1[:, m : m + 1],
-                    scale=1.0,
-                )
+            hps = ph.tile([P, 512], F32, tag="h")
+            hpss[(n, m)] = hps
+            nc.tensor.matmul_mx(
+                out=hps[:],
+                lhsT=w1cod[:, m * P : (m + 1) * P].bitcast(FP8X4),
+                lhsT_scale=w1scl[:, m * P : (m + 1) * P],
+                rhs=acod[:].bitcast(FP8X4),
+                rhs_scale=ascl[:],
+                start=True,
+                stop=True,
+            )
 
-        def regroup_h(n, br):
+        def op_relu(n, m):
+            br, t = m // 4, m % 4
+            if t == 0:
+                hpl = two.tile([P, 4, 512], BF16, tag="hpl%d" % br)
+                hpls[(n, br)] = hpl
+            nc.scalar.activation(
+                out=hpls[(n, br)][:, t, :],
+                in_=hpss[(n, m)][:],
+                func=ACT.Relu,
+                bias=bias[:, m : m + 1],
+                scale=1.0,
+            )
+
+        def op_rg(n, br):
             hg = two.tile([P, 512, 4], BF16, tag="hg%d" % br, align_bytes=64)
             regroup(hg, hpls[(n, br)])
             hgs[(n, br)] = hg
 
-        def quant_h(n, br):
+        def op_qh(n, br):
             hcod = two.tile([P, 512], U32, tag="hcod%d" % br, align_bytes=64)
             hscl = two.tile([P, 512], U8, tag="hscl%d" % br, align_bytes=64)
             quant(hcod[:], hscl[:], hgs[(n, br)])
             hcods[(n, br)] = (hcod, hscl)
 
-        def stage_c1(n, k):
-            i = n * RT + k
+        def op_mxt(n, c):
+            hcod, hscl = hcods[(n, 1)]
+            tps_ = ph.tile([P, 512], F32, tag="h")
+            tpss[(n, c)] = tps_
+            nc.tensor.matmul_mx(
+                out=tps_[:],
+                lhsT=w2cod[:, 512 + c * P : 512 + (c + 1) * P].bitcast(FP8X4),
+                lhsT_scale=w2scl[:, 512 + c * P : 512 + (c + 1) * P],
+                rhs=hcod[:].bitcast(FP8X4),
+                rhs_scale=hscl[:],
+                start=True,
+                stop=True,
+            )
+
+        def op_tev(n, c):
+            if c == 0:
+                tT = two.tile([P, 4, 512], F32, tag="tT")
+                tTs[n] = tT
+            nc.scalar.activation(
+                out=tTs[n][:, c, :],
+                in_=tpss[(n, c)][:],
+                func=ACT.Identity,
+                bias=bias[:, 8 + c : 9 + c],
+                scale=1.0,
+            )
+
+        def op_mxs(i):
+            n, k = i // RT, i % RT
             hcod, hscl = hcods[(n, 0)]
             sps = ps.tile([P, 512], F32, tag="s")
+            spss[i] = sps
             nc.tensor.matmul_mx(
                 out=sps[:],
                 lhsT=hcod[:, k * P : (k + 1) * P].bitcast(FP8X4),
@@ -198,39 +235,37 @@ def tile_affinecoupling_pa_t_kernel(
                 start=True,
                 stop=True,
             )
+
+        def op_sp(i):
             sp = three.tile([P, 512], F32, tag="sp")
+            sps_sb[i] = sp
             nc.vector.scalar_tensor_tensor(
                 out=sp[:],
-                in0=sps[:],
+                in0=spss[i][:],
                 scalar=1.0,
-                in1=b2f[:, 0, :],
+                in1=b2f[:],
                 op0=ALU.mult,
                 op1=ALU.add,
                 accum_out=ld[:, i : i + 1],
             )
+
+        def op_exp(i):
             m2 = m2s[i % NM2]
             nc.scalar.activation(
                 out=m2[:, :, 1, :],
-                in_=sp[:].rearrange("p (h j) -> p h j", h=2),
+                in_=sps_sb[i][:].rearrange("p (h j) -> p h j", h=2),
                 func=ACT.Exp,
             )
+
+        def op_m(i):
+            n, k = i // RT, i % RT
+            m2 = m2s[i % NM2]
             nc.gpsimd.tensor_tensor(
                 out=m2[:, :, 1, :], in0=m2[:, :, 1, :], in1=zq[n][:, k, 1], op=ALU.mult
             )
-            nc.gpsimd.tensor_tensor(
-                out=m2[:, :, 1, :],
-                in0=m2[:, :, 1, :],
-                in1=b2f[:, 1, :].rearrange("p (h j) -> p h j", h=2),
-                op=ALU.add,
-            )
 
-        def stage_c2(n, k):
-            i = n * RT + k
-            hcod, hscl = hcods[(n, 1)]
-            m2 = m2s[i % NM2]
-            if k == 0:
-                zo = two.tile([P, RT, D], F32, tag="zo")
-                zos[n] = zo
+        def op_at(i):
+            n, k = i // RT, i % RT
             ats = []
             for h in range(2):
                 at = pat.tile([P, 2, 256], F32, tag="at")
@@ -238,60 +273,86 @@ def tile_affinecoupling_pa_t_kernel(
                 nc.tensor.matmul(
                     out=at[:, 0, :], lhsT=ident_b[:], rhs=zq[n][:, k, 0, h], start=True, stop=True
                 )
-            for h in range(2):
-                nc.tensor.matmul_mx(
-                    out=ats[h][:, 1, :],
-                    lhsT=hcod[:, k * P : (k + 1) * P].bitcast(FP8X4),
-                    lhsT_scale=hscl[:, k * P : (k + 1) * P],
-                    rhs=w2cod[:, 512 + h * 256 : 512 + (h + 1) * 256].bitcast(FP8X4),
-                    rhs_scale=w2scl[:, 512 + h * 256 : 512 + (h + 1) * 256],
-                    start=True,
-                    stop=True,
-                )
+                for u in range(2):
+                    nc.tensor.transpose(
+                        at[:, 1, u * P : (u + 1) * P],
+                        tTs[n][:, 2 * h + u, k * P : (k + 1) * P],
+                        ident_f[:],
+                    )
+            atss[i] = ats
+
+        def op_fin(i):
+            n, k = i // RT, i % RT
+            m2 = m2s[i % NM2]
+            if k == 0:
+                zo = two.tile([P, RT, D], F32, tag="zo")
+                zos[n] = zo
             for h in range(2):
                 nc.vector.tensor_tensor(
                     out=zos[n][:, k, h * 512 : (h + 1) * 512].rearrange("p (j e) -> p j e", e=2),
-                    in0=ats[h][:].rearrange("p e j -> p j e"),
+                    in0=atss[i][h][:].rearrange("p e j -> p j e"),
                     in1=m2[:, h].rearrange("p e j -> p j e"),
                     op=ALU.add,
                 )
-            if k == RT - 1:
-                nc.sync.dma_start(out=ov[:, n * RT : (n + 1) * RT, :], in_=zos[n][:])
+            if n == ST - 1:
+                nc.sync.dma_start(out=ov[:, i : i + 1, :], in_=zos[n][:, k : k + 1, :])
+            elif k % 2 == 1:
+                nc.sync.dma_start(out=ov[:, i - 1 : i + 1, :], in_=zos[n][:, k - 1 : k + 1, :])
 
-        nslots = NT + LAG_C2
+        def m_of(k):
+            return (4 + 2 * k, 5 + 2 * k) if k < 2 else (2 * (k - 2), 2 * (k - 2) + 1)
+
+        def ok(j):
+            return 0 <= j < NT
+
+        nslots = NT + LAG["fin"] + 1
         for q in range(nslots):
-            if q < NT:
-                stage_a(q // RT, q % RT)
-            if q == 2:
-                btp = ptp.tile([P, P], BF16, tag="tp")
-                nc.tensor.transpose(btp[:], bt[:], ident_b[:])
-                nc.vector.tensor_copy(out=b1[:], in_=btp[:, 0:8])
-            if q >= 4 and q % RT == 0 and q // RT - 1 < ST:
-                quant_a(q // RT - 1)
-            if q == 4:
-                w_regroup("w2s", raw_w2s)
-            if q == 5:
-                w_regroup("w2t", raw_w2t)
-                quant(w2cod[:, 0:512], w2scl[:, 0:512], wg["w2s"])
-            if q == 6:
-                quant(w2cod[:, 512:1024], w2scl[:, 512:1024], wg["w2t"])
-                nc.vector.tensor_copy(out=b2f[:], in_=b2raw[:])
-            qb = q - LAG_B
-            if 0 <= qb < NT:
-                stage_b(qb // RT, qb % RT)
-            qc = q - LAG_C1
-            if 0 <= qc < NT:
-                stage_c1(qc // RT, qc % RT)
-            qd = q - LAG_C2
-            if 0 <= qd < NT:
-                stage_c2(qd // RT, qd % RT)
-            if 0 <= qb < NT and qb % RT == 1:
-                regroup_h(qb // RT, 0)
-            if 0 <= qb < NT and qb % RT == 2:
-                quant_h(qb // RT, 0)
-            if 0 <= qb < NT and qb % RT == 3:
-                regroup_h(qb // RT, 1)
-            if 0 <= qb - 1 < NT and (qb - 1) % RT == 3:
-                quant_h((qb - 1) // RT, 1)
+            for o in ORDER:
+                j = q - LAG[o]
+                if o == "tr" and ok(j):
+                    op_tr(j)
+                    if j == 2:
+                        btp = ptp.tile([P, P], BF16, tag="tp")
+                        nc.tensor.transpose(btp[:], bt[:], ident_b[:])
+                        nc.vector.tensor_copy(out=bias[:], in_=btp[:, 0:12])
+                elif o == "aev" and ok(j):
+                    op_aev(j)
+                elif o == "QA" and ok(j) and j % 4 == 3:
+                    op_qa(j // 4)
+                elif o == "W":
+                    if j == 0:
+                        w_regroup("w2t", raw_w2t, "hg1")
+                    elif j == 1:
+                        w_regroup("w2s", raw_w2s, "hg0")
+                        quant(w2cod[:, 512:1024], w2scl[:, 512:1024], wg["w2t"])
+                    elif j == 2:
+                        quant(w2cod[:, 0:512], w2scl[:, 0:512], wg["w2s"])
+                        nc.vector.tensor_copy(out=b2f[:], in_=b2raw[:])
+                elif o == "mx1" and ok(j):
+                    for m in m_of(j % 4):
+                        op_mx1(j // 4, m)
+                elif o == "relu" and ok(j):
+                    for m in m_of(j % 4):
+                        op_relu(j // 4, m)
+                elif o == "RG" and ok(j) and j % 2 == 1:
+                    op_rg(j // 4, 1 if j % 4 == 1 else 0)
+                elif o == "QH" and ok(j) and j % 2 == 1:
+                    op_qh(j // 4, 1 if j % 4 == 1 else 0)
+                elif o == "mxT" and ok(j):
+                    op_mxt(j // 4, j % 4)
+                elif o == "tev" and ok(j):
+                    op_tev(j // 4, j % 4)
+                elif o == "mxs" and ok(j):
+                    op_mxs(j)
+                elif o == "sp" and ok(j):
+                    op_sp(j)
+                elif o == "exp" and ok(j):
+                    op_exp(j)
+                elif o == "M" and ok(j):
+                    op_m(j)
+                elif o == "at" and ok(j):
+                    op_at(j)
+                elif o == "fin" and ok(j):
+                    op_fin(j)
 
         nc.sync.dma_start(out=ldv, in_=ld[:])

@@ -45,6 +45,8 @@ def tile_affinecoupling_pa_t_kernel(
         ps = ctx.enter_context(tc.psum_pool(name="ps", bufs=2))
         pat = ctx.enter_context(tc.psum_pool(name="pat", bufs=2))
 
+        bt = const.tile([P, P], BF16, name="bt")
+        nc.vector.memset(bt[:], 0.0)
         ident_f = const.tile([P, P], F32, name="ident_f")
         make_identity(nc, ident_f[:])
         ident_b = const.tile([P, P], BF16, name="ident_b")
@@ -52,11 +54,8 @@ def tile_affinecoupling_pa_t_kernel(
         m2s = []
         for i in range(NM2):
             m2 = const.tile([P, 2, 2, 256], F32, name="m2_%d" % i)
-            nc.gpsimd.memset(m2[:], 0.0)
             m2s.append(m2)
 
-        bt = const.tile([P, P], BF16, name="bt")
-        nc.vector.memset(bt[:], 0.0)
 
         z_sb = []
         for n in range(ST):
@@ -79,9 +78,8 @@ def tile_affinecoupling_pa_t_kernel(
         raw_w1t = load_w(W1_t, "hpl1")
         load_z(0, 2, 4)
         raw_w1s = load_w(W1_s, "hpl0")
-        nc.sync.dma_start(out=bt[0:4, :], in_=b1_s.rearrange("(t p) -> t p", p=P))
-        nc.sync.dma_start(out=bt[4:8, :], in_=b1_t.rearrange("(t p) -> t p", p=P))
-        nc.sync.dma_start(out=bt[8:12, :], in_=b2_t.rearrange("(t p) -> t p", p=P))
+        for r, b in enumerate((b1_s, b1_t, b2_t)):
+            nc.scalar.dma_start(out=bt[4 * r : 4 * r + 4, :], in_=b.rearrange("(t p) -> t p", p=P))
         load_z(1, 0, 4)
         raw_w2t = load_w(W2_t, "wraw")
         raw_w2s = load_w(W2_s, "wraw")
@@ -118,14 +116,19 @@ def tile_affinecoupling_pa_t_kernel(
 
         wg = {}
 
+        def clear_m2():
+            for m2 in m2s:
+                nc.gpsimd.memset(m2[:, :, 0, :], 0.0)
+
+
         def w_regroup(key, raw, tag):
             grp = two.tile([P, 512, 4], BF16, tag=tag, align_bytes=64)
             regroup(grp, raw)
             wg[key] = grp
 
         w_regroup("w1t", raw_w1t, "hg1")
-        w_regroup("w1s", raw_w1s, "hg0")
         quant(w1cod[:, 512:1024], w1scl[:, 512:1024], wg["w1t"])
+        w_regroup("w1s", raw_w1s, "hg0")
         quant(w1cod[:, 0:512], w1scl[:, 0:512], wg["w1s"])
 
         tps, ags, acods, hpss, hpls, hgs, hcods, tpss, tTs, spss, sps_sb, atss, zos = (
@@ -173,16 +176,12 @@ def tile_affinecoupling_pa_t_kernel(
 
         def op_relu(n, m):
             br, t = m // 4, m % 4
+            src = hpss[(n, m)][:]
             if t == 0:
                 hpl = two.tile([P, 4, 512], BF16, tag="hpl%d" % br)
                 hpls[(n, br)] = hpl
-            nc.scalar.activation(
-                out=hpls[(n, br)][:, t, :],
-                in_=hpss[(n, m)][:],
-                func=ACT.Relu,
-                bias=bias[:, m : m + 1],
-                scale=1.0,
-            )
+            dst = hpls[(n, br)][:, t, :]
+            nc.scalar.activation(out=dst, in_=src, func=ACT.Relu, bias=bias[:, m : m + 1], scale=1.0)
 
         def op_rg(n, br):
             hg = two.tile([P, 512, 4], BF16, tag="hg%d" % br, align_bytes=64)
@@ -213,13 +212,8 @@ def tile_affinecoupling_pa_t_kernel(
             if c == 0:
                 tT = two.tile([P, 4, 512], F32, tag="tT")
                 tTs[n] = tT
-            nc.scalar.activation(
-                out=tTs[n][:, c, :],
-                in_=tpss[(n, c)][:],
-                func=ACT.Identity,
-                bias=bias[:, 8 + c : 9 + c],
-                scale=1.0,
-            )
+            dst, src = tTs[n][:, c, :], tpss[(n, c)][:]
+            nc.scalar.activation(out=dst, in_=src, func=ACT.Identity, bias=bias[:, 8 + c : 9 + c], scale=1.0)
 
         def op_mxs(i):
             n, k = i // RT, i % RT
@@ -311,16 +305,17 @@ def tile_affinecoupling_pa_t_kernel(
                 j = q - LAG[o]
                 if o == "tr" and ok(j):
                     op_tr(j)
-                    if j == 2:
+                    if j == 1:
                         btp = ptp.tile([P, P], BF16, tag="tp")
                         nc.tensor.transpose(btp[:], bt[:], ident_b[:])
-                        nc.vector.tensor_copy(out=bias[:], in_=btp[:, 0:12])
+                        nc.scalar.copy(out=bias[:], in_=btp[:, 0:12])
                 elif o == "aev" and ok(j):
                     op_aev(j)
                 elif o == "QA" and ok(j) and j % 4 == 3:
                     op_qa(j // 4)
                 elif o == "W":
                     if j == 0:
+                        clear_m2()
                         w_regroup("w2t", raw_w2t, "hg1")
                     elif j == 1:
                         w_regroup("w2s", raw_w2s, "hg0")

@@ -49,13 +49,14 @@ def tile_affinecoupling_pa_t_kernel(
         nc.vector.memset(bt[:], 0.0)
         ident_f = const.tile([P, P], F32, name="ident_f")
         make_identity(nc, ident_f[:])
-        ident_b = const.tile([P, P], BF16, name="ident_b")
-        make_identity(nc, ident_b[:])
         m2s = []
         for i in range(NM2):
             m2 = const.tile([P, 2, 2, 256], F32, name="m2_%d" % i)
+            nc.gpsimd.memset(m2[:, :, 0, :], 0.0)
             m2s.append(m2)
 
+        ident_b = const.tile([P, P], BF16, name="ident_b")
+        make_identity(nc, ident_b[:])
 
         z_sb = []
         for n in range(ST):
@@ -74,13 +75,14 @@ def tile_affinecoupling_pa_t_kernel(
             return raw
 
         b2raw = const.tile([P, 512], BF16, name="b2raw")
+        for r, b in enumerate((b1_s, b1_t, b2_t)):
+            nc.scalar.dma_start(out=bt[4 * r : 4 * r + 4, :], in_=b.rearrange("(t p) -> t p", p=P))
         load_z(0, 0, 2)
         raw_w1t = load_w(W1_t, "hpl1")
         load_z(0, 2, 4)
         raw_w1s = load_w(W1_s, "hpl0")
-        for r, b in enumerate((b1_s, b1_t, b2_t)):
-            nc.scalar.dma_start(out=bt[4 * r : 4 * r + 4, :], in_=b.rearrange("(t p) -> t p", p=P))
-        load_z(1, 0, 4)
+        load_z(1, 0, 2)
+        load_z(1, 2, 4)
         raw_w2t = load_w(W2_t, "wraw")
         raw_w2s = load_w(W2_s, "wraw")
         nc.sync.dma_start(out=b2raw[:], in_=b2_s.partition_broadcast(P))
@@ -101,8 +103,8 @@ def tile_affinecoupling_pa_t_kernel(
         b2f = const.tile([P, 512], F32, name="b2f")
         ld = const.tile([P, NT], F32, name="ld")
 
-        def regroup(dst, src):
-            nc.vector.tensor_copy(
+        def regroup(dst, src, copy=nc.vector.tensor_copy):
+            copy(
                 out=dst[:].rearrange("p (c i) t -> p c t i", i=4),
                 in_=src[:].rearrange("p t (c i) -> p c t i", i=4),
             )
@@ -116,11 +118,6 @@ def tile_affinecoupling_pa_t_kernel(
 
         wg = {}
 
-        def clear_m2():
-            for m2 in m2s:
-                nc.gpsimd.memset(m2[:, :, 0, :], 0.0)
-
-
         def w_regroup(key, raw, tag):
             grp = two.tile([P, 512, 4], BF16, tag=tag, align_bytes=64)
             regroup(grp, raw)
@@ -128,8 +125,6 @@ def tile_affinecoupling_pa_t_kernel(
 
         w_regroup("w1t", raw_w1t, "hg1")
         quant(w1cod[:, 512:1024], w1scl[:, 512:1024], wg["w1t"])
-        w_regroup("w1s", raw_w1s, "hg0")
-        quant(w1cod[:, 0:512], w1scl[:, 0:512], wg["w1s"])
 
         tps, ags, acods, hpss, hpls, hgs, hcods, tpss, tTs, spss, sps_sb, atss, zos = (
             {}, {}, {}, {}, {}, {}, {}, {}, {}, {}, {}, {}, {},
@@ -185,7 +180,7 @@ def tile_affinecoupling_pa_t_kernel(
 
         def op_rg(n, br):
             hg = two.tile([P, 512, 4], BF16, tag="hg%d" % br, align_bytes=64)
-            regroup(hg, hpls[(n, br)])
+            regroup(hg, hpls[(n, br)], nc.scalar.copy if (n, br) == (ST - 1, 0) else nc.vector.tensor_copy)
             hgs[(n, br)] = hg
 
         def op_qh(n, br):
@@ -305,7 +300,7 @@ def tile_affinecoupling_pa_t_kernel(
                 j = q - LAG[o]
                 if o == "tr" and ok(j):
                     op_tr(j)
-                    if j == 1:
+                    if j == 3:
                         btp = ptp.tile([P, P], BF16, tag="tp")
                         nc.tensor.transpose(btp[:], bt[:], ident_b[:])
                         nc.scalar.copy(out=bias[:], in_=btp[:, 0:12])
@@ -313,14 +308,17 @@ def tile_affinecoupling_pa_t_kernel(
                     op_aev(j)
                 elif o == "QA" and ok(j) and j % 4 == 3:
                     op_qa(j // 4)
+                    if j == RT - 1:
+                        w_regroup("w1s", raw_w1s, "hg0")
+                        quant(w1cod[:, 0:512], w1scl[:, 0:512], wg["w1s"])
                 elif o == "W":
                     if j == 0:
-                        clear_m2()
                         w_regroup("w2t", raw_w2t, "hg1")
-                    elif j == 1:
+                    if j == 1:
                         w_regroup("w2s", raw_w2s, "hg0")
+                    if j == 1:
                         quant(w2cod[:, 512:1024], w2scl[:, 512:1024], wg["w2t"])
-                    elif j == 2:
+                    if j == 2:
                         quant(w2cod[:, 0:512], w2scl[:, 0:512], wg["w2s"])
                         nc.vector.tensor_copy(out=b2f[:], in_=b2raw[:])
                 elif o == "mx1" and ok(j):

@@ -41,8 +41,8 @@ def tile_affinecoupling_pa_t_kernel(
         two = ctx.enter_context(tc.tile_pool(name="two", bufs=2))
         three = ctx.enter_context(tc.tile_pool(name="three", bufs=3))
         ptp = ctx.enter_context(tc.psum_pool(name="ptp", bufs=2))
-        ph = ctx.enter_context(tc.psum_pool(name="ph", bufs=2))
-        ps = ctx.enter_context(tc.psum_pool(name="ps", bufs=2))
+        ph = ctx.enter_context(tc.psum_pool(name="ph", bufs=3))
+        ps = ctx.enter_context(tc.psum_pool(name="ps", bufs=1))
         pat = ctx.enter_context(tc.psum_pool(name="pat", bufs=2))
 
         bt = const.tile([P, P], BF16, name="bt")

@@ -21,10 +21,10 @@ ST = NT // RT
 NM2 = 4
 
 LAG = {
-    "tr": 0, "aev": 0, "QA": 1, "W": 4, "mx1": 5, "relu": 5, "RG": 5, "QH": 6,
-    "mxT": 8, "tev": 8, "mxs": 10, "sp": 10, "exp": 10, "M": 11, "at": 13, "fin": 13,
+    "tr": 0, "aev": 0, "QA": 0, "W": 4, "mx1": 4, "relu": 5, "RG": 5, "QH": 6,
+    "mxT": 8, "tev": 8, "mxs": 10, "sp": 10, "exp": 10, "M": 11, "at": 12, "fin": 13,
 }
-ORDER = ["QA", "at", "tr", "mx1", "mxs", "relu", "fin", "mxT", "M", "sp", "RG", "W", "aev", "QH", "tev", "exp"]
+ORDER = ["M", "relu", "fin", "tr", "aev", "mxs", "sp", "mxT", "tev", "exp", "RG", "QH", "QA", "W", "mx1", "at"]
 
 
 def tile_affinecoupling_pa_t_kernel(
@@ -103,8 +103,8 @@ def tile_affinecoupling_pa_t_kernel(
         b2f = const.tile([P, 512], F32, name="b2f")
         ld = const.tile([P, NT], F32, name="ld")
 
-        def regroup(dst, src, copy=nc.vector.tensor_copy):
-            copy(
+        def regroup(dst, src):
+            nc.vector.tensor_copy(
                 out=dst[:].rearrange("p (c i) t -> p c t i", i=4),
                 in_=src[:].rearrange("p t (c i) -> p c t i", i=4),
             )
@@ -180,7 +180,7 @@ def tile_affinecoupling_pa_t_kernel(
 
         def op_rg(n, br):
             hg = two.tile([P, 512, 4], BF16, tag="hg%d" % br, align_bytes=64)
-            regroup(hg, hpls[(n, br)], nc.scalar.copy if (n, br) == (ST - 1, 0) else nc.vector.tensor_copy)
+            regroup(hg, hpls[(n, br)])
             hgs[(n, br)] = hg
 
         def op_qh(n, br):

@@ -176,7 +176,12 @@ def tile_affinecoupling_pa_t_kernel(
                 hpl = two.tile([P, 4, 512], BF16, tag="hpl%d" % br)
                 hpls[(n, br)] = hpl
             dst = hpls[(n, br)][:, t, :]
-            nc.scalar.activation(out=dst, in_=src, func=ACT.Relu, bias=bias[:, m : m + 1], scale=1.0)
+            if n == 1 and m % 2 == 1:
+                nc.vector.tensor_scalar(
+                    out=dst, in0=src, scalar1=bias[:, m : m + 1], scalar2=0.0, op0=ALU.add, op1=ALU.max
+                )
+            else:
+                nc.scalar.activation(out=dst, in_=src, func=ACT.Relu, bias=bias[:, m : m + 1], scale=1.0)
 
         def op_rg(n, br):
             hg = two.tile([P, 512, 4], BF16, tag="hg%d" % br, align_bytes=64)
@@ -300,16 +305,17 @@ def tile_affinecoupling_pa_t_kernel(
                 j = q - LAG[o]
                 if o == "tr" and ok(j):
                     op_tr(j)
+                elif o == "aev" and ok(j):
+                    op_aev(j)
                     if j == 3:
                         btp = ptp.tile([P, P], BF16, tag="tp")
                         nc.tensor.transpose(btp[:], bt[:], ident_b[:])
                         nc.scalar.copy(out=bias[:], in_=btp[:, 0:12])
-                elif o == "aev" and ok(j):
-                    op_aev(j)
                 elif o == "QA" and ok(j) and j % 4 == 3:
-                    op_qa(j // 4)
                     if j == RT - 1:
                         w_regroup("w1s", raw_w1s, "hg0")
+                    op_qa(j // 4)
+                    if j == RT - 1:
                         quant(w1cod[:, 0:512], w1scl[:, 0:512], wg["w1s"])
                 elif o == "W":
                     if j == 0:

@@ -81,10 +81,11 @@ def tile_affinecoupling_pa_t_kernel(
         raw_w1t = load_w(W1_t, "hpl1")
         load_z(0, 2, 4)
         raw_w1s = load_w(W1_s, "hpl0")
-        load_z(1, 0, 2)
-        load_z(1, 2, 4)
+        load_z(1, 0, 1)
         raw_w2t = load_w(W2_t, "wraw")
+        load_z(1, 1, 2)
         raw_w2s = load_w(W2_s, "wraw")
+        load_z(1, 2, 4)
         nc.sync.dma_start(out=b2raw[:], in_=b2_s.partition_broadcast(P))
         for n in range(2, ST):
             load_z(n, 0, 4)
@@ -176,12 +177,7 @@ def tile_affinecoupling_pa_t_kernel(
                 hpl = two.tile([P, 4, 512], BF16, tag="hpl%d" % br)
                 hpls[(n, br)] = hpl
             dst = hpls[(n, br)][:, t, :]
-            if n == 1 and m % 2 == 1:
-                nc.vector.tensor_scalar(
-                    out=dst, in0=src, scalar1=bias[:, m : m + 1], scalar2=0.0, op0=ALU.add, op1=ALU.max
-                )
-            else:
-                nc.scalar.activation(out=dst, in_=src, func=ACT.Relu, bias=bias[:, m : m + 1], scale=1.0)
+            nc.scalar.activation(out=dst, in_=src, func=ACT.Relu, bias=bias[:, m : m + 1], scale=1.0)
 
         def op_rg(n, br):
             hg = two.tile([P, 512, 4], BF16, tag="hg%d" % br, align_bytes=64)
@@ -288,6 +284,12 @@ def tile_affinecoupling_pa_t_kernel(
                     in1=m2[:, h].rearrange("p e j -> p j e"),
                     op=ALU.add,
                 )
+                if i == NT - 1:
+                    nc.sync.dma_start(
+                        out=ov[:, i, h * 512 : (h + 1) * 512], in_=zos[n][:, k, h * 512 : (h + 1) * 512]
+                    )
+            if i == NT - 1:
+                return
             if n == ST - 1:
                 nc.sync.dma_start(out=ov[:, i : i + 1, :], in_=zos[n][:, k : k + 1, :])
             elif k % 2 == 1:
@@ -345,6 +347,8 @@ def tile_affinecoupling_pa_t_kernel(
                     op_mxs(j)
                 elif o == "sp" and ok(j):
                     op_sp(j)
+                    if j == NT - 1:
+                        nc.sync.dma_start(out=ldv, in_=ld[:])
                 elif o == "exp" and ok(j):
                     op_exp(j)
                 elif o == "M" and ok(j):
@@ -353,5 +357,3 @@ def tile_affinecoupling_pa_t_kernel(
                     op_at(j)
                 elif o == "fin" and ok(j):
                     op_fin(j)
-
-        nc.sync.dma_start(out=ldv, in_=ld[:])

@@ -177,7 +177,12 @@ def tile_affinecoupling_pa_t_kernel(
                 hpl = two.tile([P, 4, 512], BF16, tag="hpl%d" % br)
                 hpls[(n, br)] = hpl
             dst = hpls[(n, br)][:, t, :]
-            nc.scalar.activation(out=dst, in_=src, func=ACT.Relu, bias=bias[:, m : m + 1], scale=1.0)
+            if n == 1 and m % 2 == 1:
+                nc.vector.tensor_scalar(
+                    out=dst, in0=src, scalar1=bias[:, m : m + 1], scalar2=0.0, op0=ALU.add, op1=ALU.max
+                )
+            else:
+                nc.scalar.activation(out=dst, in_=src, func=ACT.Relu, bias=bias[:, m : m + 1], scale=1.0)
 
         def op_rg(n, br):
             hg = two.tile([P, 512, 4], BF16, tag="hg%d" % br, align_bytes=64)

@@ -106,8 +106,8 @@ def tile_affinecoupling_pa_t_kernel(
 
         def regroup(dst, src):
             nc.vector.tensor_copy(
-                out=dst[:].rearrange("p (c i) t -> p c t i", i=4),
-                in_=src[:].rearrange("p t (c i) -> p c t i", i=4),
+                out=dst[:].rearrange("p (c i) t -> p c t i", i=8),
+                in_=src[:].rearrange("p t (c i) -> p c t i", i=8),
             )
 
         def quant(cod, scl, grp):

@@ -104,11 +104,13 @@ def tile_affinecoupling_pa_t_kernel(
         b2f = const.tile([P, 512], F32, name="b2f")
         ld = const.tile([P, NT], F32, name="ld")
 
-        def regroup(dst, src):
-            nc.vector.tensor_copy(
-                out=dst[:].rearrange("p (c i) t -> p c t i", i=8),
-                in_=src[:].rearrange("p t (c i) -> p c t i", i=8),
-            )
+        def regroup(dst, src, cut=0):
+            for copy, a, b in ((nc.scalar.copy, 0, cut), (nc.vector.tensor_copy, cut, 512)):
+                if a < b:
+                    copy(
+                        out=dst[:, a:b, :].rearrange("p (c i) t -> p c t i", i=8),
+                        in_=src[:, :, a:b].rearrange("p t (c i) -> p c t i", i=8),
+                    )
 
         def quant(cod, scl, grp):
             nc.vector.quantize_mx(
@@ -186,7 +188,7 @@ def tile_affinecoupling_pa_t_kernel(
 
         def op_rg(n, br):
             hg = two.tile([P, 512, 4], BF16, tag="hg%d" % br, align_bytes=64)
-            regroup(hg, hpls[(n, br)])
+            regroup(hg, hpls[(n, br)], 160 if (n, br) == (ST - 1, 0) else 0)
             hgs[(n, br)] = hg
 
         def op_qh(n, br):

from contextlib import ExitStack

import concourse.mybir as mybir
from concourse.masks import make_identity

FLOPS = 4 * 2 * 4096 * 512 * 512

FP8X4 = mybir.dt.float8_e4m3fn_x4
BF16 = mybir.dt.bfloat16
F32 = mybir.dt.float32
U32 = mybir.dt.uint32
U8 = mybir.dt.uint8
ACT = mybir.ActivationFunctionType
ALU = mybir.AluOpType

P = 128
D = 1024
NT = 32
RT = 4
ST = NT // RT
NM2 = 4

LAG = {
    "tr": 0, "aev": 0, "QA": 0, "W": 4, "mx1": 4, "relu": 5, "RG": 5, "QH": 6,
    "mxT": 8, "tev": 8, "mxs": 10, "sp": 10, "exp": 10, "M": 11, "at": 12, "fin": 13,
}
ORDER = ["M", "relu", "fin", "tr", "aev", "mxs", "sp", "mxT", "tev", "exp", "RG", "QH", "QA", "W", "mx1", "at"]


def tile_affinecoupling_pa_t_kernel(
    tc, z, W1_s, b1_s, W2_s, b2_s, W1_t, b1_t, W2_t, b2_t, out_0, out_1
):
    nc = tc.nc
    zv = z.rearrange("(p i) d -> p i d", i=NT)
    ov = out_0.rearrange("(p i) d -> p i d", i=NT)
    ldv = out_1.rearrange("(p i) -> p i", i=NT)

    with ExitStack() as ctx:
        ctx.enter_context(tc.manual_schedule())
        const = ctx.enter_context(tc.tile_pool(name="const", bufs=1))
        two = ctx.enter_context(tc.tile_pool(name="two", bufs=2))
        three = ctx.enter_context(tc.tile_pool(name="three", bufs=3))
        ptp = ctx.enter_context(tc.psum_pool(name="ptp", bufs=2))
        ph = ctx.enter_context(tc.psum_pool(name="ph", bufs=3))
        ps = ctx.enter_context(tc.psum_pool(name="ps", bufs=1))
        pat = ctx.enter_context(tc.psum_pool(name="pat", bufs=2))

        bt = const.tile([P, P], BF16, name="bt")
        nc.vector.memset(bt[:], 0.0)
        ident_f = const.tile([P, P], F32, name="ident_f")
        make_identity(nc, ident_f[:])
        m2s = []
        for i in range(NM2):
            m2 = const.tile([P, 2, 2, 256], F32, name="m2_%d" % i)
            nc.gpsimd.memset(m2[:, :, 0, :], 0.0)
            m2s.append(m2)

        ident_b = const.tile([P, P], BF16, name="ident_b")
        make_identity(nc, ident_b[:])

        z_sb = []
        for n in range(ST):
            zt = const.tile([P, RT * D], BF16, name="z%d" % n)
            z_sb.append(zt)

        def load_z(n, lo, hi):
            nc.sync.dma_start(
                out=z_sb[n][:, lo * D : hi * D].rearrange("p (i d) -> p i d", d=D),
                in_=zv[:, n * RT + lo : n * RT + hi, :],
            )

        def load_w(w, tag):
            raw = two.tile([P, 4, 512], BF16, tag=tag)
            nc.sync.dma_start(out=raw[:], in_=w.rearrange("(c p) n -> p c n", p=P))
            return raw

        b2raw = const.tile([P, 512], BF16, name="b2raw")
        for r, b in enumerate((b1_s, b1_t, b2_t)):
            nc.scalar.dma_start(out=bt[4 * r : 4 * r + 4, :], in_=b.rearrange("(t p) -> t p", p=P))
        load_z(0, 0, 2)
        raw_w1t = load_w(W1_t, "hpl1")
        load_z(0, 2, 4)
        raw_w1s = load_w(W1_s, "hpl0")
        load_z(1, 0, 1)
        raw_w2t = load_w(W2_t, "wraw")
        load_z(1, 1, 2)
        raw_w2s = load_w(W2_s, "wraw")
        load_z(1, 2, 4)
        nc.sync.dma_start(out=b2raw[:], in_=b2_s.partition_broadcast(P))
        for n in range(2, ST):
            load_z(n, 0, 4)

        zw = [t[:].bitcast(F32) for t in z_sb]
        zq = [
            t[:].rearrange("p (r h j e) -> p r e h j", r=RT, h=2, j=256, e=2)
            for t in z_sb
        ]

        w1cod = const.tile([P, 1024], U32, name="w1cod", align_bytes=64)
        w1scl = const.tile([P, 1024], U8, name="w1scl", align_bytes=64)
        w2cod = const.tile([P, 1024], U32, name="w2cod", align_bytes=64)
        w2scl = const.tile([P, 1024], U8, name="w2scl", align_bytes=64)
        bias = const.tile([P, 12], F32, name="bias")
        b2f = const.tile([P, 512], F32, name="b2f")
        ld = const.tile([P, NT], F32, name="ld")

        def regroup(dst, src, cut=0):
            for copy, a, b in ((nc.scalar.copy, 0, cut), (nc.vector.tensor_copy, cut, 512)):
                if a < b:
                    copy(
                        out=dst[:, a:b, :].rearrange("p (c i) t -> p c t i", i=8),
                        in_=src[:, :, a:b].rearrange("p t (c i) -> p c t i", i=8),
                    )

        def quant(cod, scl, grp):
            nc.vector.quantize_mx(
                out=cod.bitcast(FP8X4),
                scales=scl,
                in_=grp[:].rearrange("p w t -> p (w t)"),
            )

        wg = {}

        def w_regroup(key, raw, tag):
            grp = two.tile([P, 512, 4], BF16, tag=tag, align_bytes=64)
            regroup(grp, raw)
            wg[key] = grp

        w_regroup("w1t", raw_w1t, "hg1")
        quant(w1cod[:, 512:1024], w1scl[:, 512:1024], wg["w1t"])

        tps, ags, acods, hpss, hpls, hgs, hcods, tpss, tTs, spss, sps_sb, atss, zos = (
            {}, {}, {}, {}, {}, {}, {}, {}, {}, {}, {}, {}, {},
        )

        def op_tr(i):
            n, k = i // RT, i % RT
            tp = ptp.tile([P, 512], F32, tag="tp")
            tps[i] = tp
            for c in range(4):
                nc.tensor.transpose(
                    tp[:, c * P : (c + 1) * P],
                    zw[n][:, k * 512 + c * P : k * 512 + (c + 1) * P],
                    ident_f[:],
                )

        def op_aev(i):
            n, k = i // RT, i % RT
            if k == 0:
                ag = two.tile([P, 512, 4], BF16, tag="ag", align_bytes=64)
                ags[n] = ag
            src = tps[i][:].bitcast(BF16).rearrange("p (c w e) -> p e w c", c=4, w=P, e=2)
            nc.scalar.copy(out=ags[n][:, k * P : (k + 1) * P, :], in_=src[:, 0])

        def op_qa(n):
            acod = two.tile([P, 512], U32, tag="acod", align_bytes=64)
            ascl = two.tile([P, 512], U8, tag="ascl", align_bytes=64)
            quant(acod[:], ascl[:], ags[n])
            acods[n] = (acod, ascl)

        def op_mx1(n, m):
            acod, ascl = acods[n]
            hps = ph.tile([P, 512], F32, tag="h")
            hpss[(n, m)] = hps
            nc.tensor.matmul_mx(
                out=hps[:],
                lhsT=w1cod[:, m * P : (m + 1) * P].bitcast(FP8X4),
                lhsT_scale=w1scl[:, m * P : (m + 1) * P],
                rhs=acod[:].bitcast(FP8X4),
                rhs_scale=ascl[:],
                start=True,
                stop=True,
            )

        def op_relu(n, m):
            br, t = m // 4, m % 4
            src = hpss[(n, m)][:]
            if t == 0:
                hpl = two.tile([P, 4, 512], BF16, tag="hpl%d" % br)
                hpls[(n, br)] = hpl
            dst = hpls[(n, br)][:, t, :]
            if n == 1 and m % 2 == 1:
                nc.vector.tensor_scalar(
                    out=dst, in0=src, scalar1=bias[:, m : m + 1], scalar2=0.0, op0=ALU.add, op1=ALU.max
                )
            else:
                nc.scalar.activation(out=dst, in_=src, func=ACT.Relu, bias=bias[:, m : m + 1], scale=1.0)

        def op_rg(n, br):
            hg = two.tile([P, 512, 4], BF16, tag="hg%d" % br, align_bytes=64)
            regroup(hg, hpls[(n, br)], 160 if (n, br) == (ST - 1, 0) else 0)
            hgs[(n, br)] = hg

        def op_qh(n, br):
            hcod = two.tile([P, 512], U32, tag="hcod%d" % br, align_bytes=64)
            hscl = two.tile([P, 512], U8, tag="hscl%d" % br, align_bytes=64)
            quant(hcod[:], hscl[:], hgs[(n, br)])
            hcods[(n, br)] = (hcod, hscl)

        def op_mxt(n, c):
            hcod, hscl = hcods[(n, 1)]
            tps_ = ph.tile([P, 512], F32, tag="h")
            tpss[(n, c)] = tps_
            nc.tensor.matmul_mx(
                out=tps_[:],
                lhsT=w2cod[:, 512 + c * P : 512 + (c + 1) * P].bitcast(FP8X4),
                lhsT_scale=w2scl[:, 512 + c * P : 512 + (c + 1) * P],
                rhs=hcod[:].bitcast(FP8X4),
                rhs_scale=hscl[:],
                start=True,
                stop=True,
            )

        def op_tev(n, c):
            if c == 0:
                tT = two.tile([P, 4, 512], F32, tag="tT")
                tTs[n] = tT
            dst, src = tTs[n][:, c, :], tpss[(n, c)][:]
            nc.scalar.activation(out=dst, in_=src, func=ACT.Identity, bias=bias[:, 8 + c : 9 + c], scale=1.0)

        def op_mxs(i):
            n, k = i // RT, i % RT
            hcod, hscl = hcods[(n, 0)]
            sps = ps.tile([P, 512], F32, tag="s")
            spss[i] = sps
            nc.tensor.matmul_mx(
                out=sps[:],
                lhsT=hcod[:, k * P : (k + 1) * P].bitcast(FP8X4),
                lhsT_scale=hscl[:, k * P : (k + 1) * P],
                rhs=w2cod[:, 0:512].bitcast(FP8X4),
                rhs_scale=w2scl[:, 0:512],
                start=True,
                stop=True,
            )

        def op_sp(i):
            sp = three.tile([P, 512], F32, tag="sp")
            sps_sb[i] = sp
            nc.vector.scalar_tensor_tensor(
                out=sp[:],
                in0=spss[i][:],
                scalar=1.0,
                in1=b2f[:],
                op0=ALU.mult,
                op1=ALU.add,
                accum_out=ld[:, i : i + 1],
            )

        def op_exp(i):
            m2 = m2s[i % NM2]
            nc.scalar.activation(
                out=m2[:, :, 1, :],
                in_=sps_sb[i][:].rearrange("p (h j) -> p h j", h=2),
                func=ACT.Exp,
            )

        def op_m(i):
            n, k = i // RT, i % RT
            m2 = m2s[i % NM2]
            nc.gpsimd.tensor_tensor(
                out=m2[:, :, 1, :], in0=m2[:, :, 1, :], in1=zq[n][:, k, 1], op=ALU.mult
            )

        def op_at(i):
            n, k = i // RT, i % RT
            ats = []
            for h in range(2):
                at = pat.tile([P, 2, 256], F32, tag="at")
                ats.append(at)
                nc.tensor.matmul(
                    out=at[:, 0, :], lhsT=ident_b[:], rhs=zq[n][:, k, 0, h], start=True, stop=True
                )
                for u in range(2):
                    nc.tensor.transpose(
                        at[:, 1, u * P : (u + 1) * P],
                        tTs[n][:, 2 * h + u, k * P : (k + 1) * P],
                        ident_f[:],
                    )
            atss[i] = ats

        def op_fin(i):
            n, k = i // RT, i % RT
            m2 = m2s[i % NM2]
            if k == 0:
                zo = two.tile([P, RT, D], F32, tag="zo")
                zos[n] = zo
            for h in range(2):
                nc.vector.tensor_tensor(
                    out=zos[n][:, k, h * 512 : (h + 1) * 512].rearrange("p (j e) -> p j e", e=2),
                    in0=atss[i][h][:].rearrange("p e j -> p j e"),
                    in1=m2[:, h].rearrange("p e j -> p j e"),
                    op=ALU.add,
                )
                if i == NT - 1:
                    nc.sync.dma_start(
                        out=ov[:, i, h * 512 : (h + 1) * 512], in_=zos[n][:, k, h * 512 : (h + 1) * 512]
                    )
            if i == NT - 1:
                return
            if n == ST - 1:
                nc.sync.dma_start(out=ov[:, i : i + 1, :], in_=zos[n][:, k : k + 1, :])
            elif k % 2 == 1:
                nc.sync.dma_start(out=ov[:, i - 1 : i + 1, :], in_=zos[n][:, k - 1 : k + 1, :])

        def m_of(k):
            return (4 + 2 * k, 5 + 2 * k) if k < 2 else (2 * (k - 2), 2 * (k - 2) + 1)

        def ok(j):
            return 0 <= j < NT

        nslots = NT + LAG["fin"] + 1
        for q in range(nslots):
            for o in ORDER:
                j = q - LAG[o]
                if o == "tr" and ok(j):
                    op_tr(j)
                elif o == "aev" and ok(j):
                    op_aev(j)
                    if j == 3:
                        btp = ptp.tile([P, P], BF16, tag="tp")
                        nc.tensor.transpose(btp[:], bt[:], ident_b[:])
                        nc.scalar.copy(out=bias[:], in_=btp[:, 0:12])
                elif o == "QA" and ok(j) and j % 4 == 3:
                    if j == RT - 1:
                        w_regroup("w1s", raw_w1s, "hg0")
                    op_qa(j // 4)
                    if j == RT - 1:
                        quant(w1cod[:, 0:512], w1scl[:, 0:512], wg["w1s"])
                elif o == "W":
                    if j == 0:
                        w_regroup("w2t", raw_w2t, "hg1")
                    if j == 1:
                        w_regroup("w2s", raw_w2s, "hg0")
                    if j == 1:
                        quant(w2cod[:, 512:1024], w2scl[:, 512:1024], wg["w2t"])
                    if j == 2:
                        quant(w2cod[:, 0:512], w2scl[:, 0:512], wg["w2s"])
                        nc.vector.tensor_copy(out=b2f[:], in_=b2raw[:])
                elif o == "mx1" and ok(j):
                    for m in m_of(j % 4):
                        op_mx1(j // 4, m)
                elif o == "relu" and ok(j):
                    for m in m_of(j % 4):
                        op_relu(j // 4, m)
                elif o == "RG" and ok(j) and j % 2 == 1:
                    op_rg(j // 4, 1 if j % 4 == 1 else 0)
                elif o == "QH" and ok(j) and j % 2 == 1:
                    op_qh(j // 4, 1 if j % 4 == 1 else 0)
                elif o == "mxT" and ok(j):
                    op_mxt(j // 4, j % 4)
                elif o == "tev" and ok(j):
                    op_tev(j // 4, j % 4)
                elif o == "mxs" and ok(j):
                    op_mxs(j)
                elif o == "sp" and ok(j):
                    op_sp(j)
                    if j == NT - 1:
                        nc.sync.dma_start(out=ldv, in_=ld[:])
                elif o == "exp" and ok(j):
                    op_exp(j)
                elif o == "M" and ok(j):
                    op_m(j)
                elif o == "at" and ok(j):
                    op_at(j)
                elif o == "fin" and ok(j):
                    op_fin(j)
